import numpy as np
import ml_dtypes


def mxq(x, axis, fmt="e4m3"):
    dtype, down = {"e4m3": (ml_dtypes.float8_e4m3fn, 7), "e5m2": (ml_dtypes.float8_e5m2, 14)}[fmt]
    v = np.moveaxis(np.asarray(x, np.float32).astype(ml_dtypes.bfloat16).astype(np.float64), axis, -1)
    blocks = v.reshape(v.shape[:-1] + (-1, 32))
    amax = np.abs(blocks).max(-1, keepdims=True)
    byte = np.maximum(np.where(amax > 0, np.frexp(amax)[1] - 1 + 127, 0) - down, 1)
    scale = np.exp2(byte - 127.0)
    codes = (blocks / scale).astype(np.float32).astype(dtype).astype(np.float64)
    return np.moveaxis((codes * scale).reshape(v.shape), -1, axis)


WIDE = False


def mx_kscale(k):
    if not WIDE:
        return np.ones(k)
    levels = np.array([10, -10, 5, -5, 0])
    a = np.random.permutation(np.resize(levels, k // 512 * 4)).reshape(k // 512, 4)
    idx = np.arange(k)
    return np.exp2(a[idx // 512, idx % 128 // 32])


BF16 = ml_dtypes.bfloat16


def bf(x):
    return np.asarray(x, np.float32).astype(BF16)


def f64(x):
    return np.asarray(x).astype(np.float64)


B, T, D, N, M = 4, 128, 1024, 2048, 512
EPS = 1e-12


def softmax(v):
    e = np.exp(v - v.max(-1, keepdims=True))
    return e / e.sum(-1, keepdims=True)


def l2n(v):
    return v * (1.0 / np.sqrt(np.maximum((v * v).sum(-1, keepdims=True), EPS)))


def setup_inputs():
    s = mx_kscale(D)
    return {"controller_output": bf(np.random.standard_normal((B, T, D)) * s),
            "Wk": bf(np.random.standard_normal((D, M)) / np.sqrt(D) / s[:, None]),
            "bk": bf(np.random.standard_normal(M) * 0.5),
            "memory": bf(np.random.standard_normal((N, M)) * 0.5 / N)}


def reference(controller_output, Wk, bk, memory):
    z = (mxq(f64(controller_output), 2, "e4m3") @ mxq(f64(Wk), 0, "e4m3")) + f64(bk)
    kn = l2n(softmax(z))
    mn = l2n(f64(memory))
    sims = -(mxq(kn, 2, "e4m3") @ mxq(mn, 1, "e4m3").T)
    return softmax(sims)

@@ -1,0 +1,318 @@
+import concourse.mybir as mybir
+from concourse.masks import make_identity
+
+F32 = mybir.dt.float32
+BF16 = mybir.dt.bfloat16
+U32 = mybir.dt.uint32
+U8 = mybir.dt.uint8
+FP8X4 = mybir.dt.float8_e4m3fn_x4
+ALU = mybir.AluOpType
+ACT = mybir.ActivationFunctionType
+AXIS_X = mybir.AxisListType.X
+
+P = 128
+TOKENS = 512
+D_IN = 1024
+D_KEY = 512
+SLOTS = 2048
+K_PASS = 512
+N_PASS = 512
+TOKEN_TILES = TOKENS // P
+X_PASSES = D_IN // K_PASS
+SLOT_TILES = SLOTS // P
+CHUNKS = SLOTS // N_PASS
+TILES_PER_CHUNK = N_PASS // P
+HALF = SLOTS // 2
+EPS = 1e-12
+
+FLOPS = 2 * TOKENS * D_IN * D_KEY + 2 * TOKENS * D_KEY * SLOTS
+
+
+def tile_contentaddressablewritehead_pa_kernel(tc, controller_output, Wk, bk, memory, out):
+    nc = tc.nc
+    x_rows = controller_output.flatten_outer_dims()
+    out_rows = out.flatten_outer_dims()
+
+    with tc.tile_pool(name="keep", bufs=1) as keep, tc.tile_pool(name="junk", bufs=4) as junk, tc.psum_pool(
+        name="psum", bufs=8
+    ) as psum:
+
+        warm = keep.tile([P, 2], F32)
+        ident = keep.tile([P, P], F32)
+        ones = keep.tile([P, P], BF16)
+        minus_half = keep.tile([P, TILES_PER_CHUNK], F32)
+        bias_rows = keep.tile([P, D_KEY], BF16)
+        neg_bias = keep.tile([P, D_KEY], F32)
+
+        x_sb = keep.tile([P, TOKEN_TILES, D_IN], BF16)
+        x_grouped = keep.tile([P, TOKEN_TILES, X_PASSES, P, 2], F32, align_bytes=64)
+        x_codes = keep.tile([P, TOKEN_TILES, X_PASSES * P], U32, align_bytes=64)
+        x_scales = keep.tile([P, TOKEN_TILES, X_PASSES * P], U8, align_bytes=64)
+
+        w_raw = keep.tile([P, X_PASSES, 4, D_KEY], BF16)
+        w_grouped = keep.tile([P, X_PASSES, D_KEY, 4], BF16, align_bytes=64)
+        w_codes = keep.tile([P, X_PASSES, D_KEY], U32, align_bytes=64)
+        w_scales = keep.tile([P, X_PASSES, D_KEY], U8, align_bytes=64)
+
+        neg_z = keep.tile([P, TOKEN_TILES, D_KEY], F32)
+        neg_z_min = keep.tile([P, TOKEN_TILES], F32)
+        e_key = keep.tile([P, TOKEN_TILES, D_KEY], F32)
+        k_sumsq = keep.tile([P, TOKEN_TILES], F32)
+        k_rnorm = keep.tile([P, TOKEN_TILES], F32)
+        kn = keep.tile([P, TOKEN_TILES, D_KEY], BF16)
+        k_grouped = keep.tile([P, TOKEN_TILES, P, 2], F32, align_bytes=64)
+        k_codes = keep.tile([P, TOKEN_TILES, P], U32, align_bytes=64)
+        k_scales = keep.tile([P, TOKEN_TILES, P], U8, align_bytes=64)
+
+        mem_sb = keep.tile([P, SLOT_TILES, D_KEY], BF16)
+        m_sumsq = keep.tile([P, SLOT_TILES], F32)
+        m_floor = keep.tile([P, SLOT_TILES], F32)
+        m_rnorm = keep.tile([P, SLOT_TILES], F32)
+        mn = keep.tile([P, SLOT_TILES, D_KEY], BF16)
+        m_grouped = keep.tile([P, SLOTS, 2], F32, align_bytes=64)
+        m_codes = keep.tile([P, SLOTS], U32, align_bytes=64)
+        m_scales = keep.tile([P, SLOTS], U8, align_bytes=64)
+
+        bank_min = keep.tile([P, TOKEN_TILES, CHUNKS], F32)
+        sims_min = keep.tile([P, TOKEN_TILES], F32)
+        bank_sum = keep.tile([P, TOKEN_TILES, CHUNKS], F32)
+        row_sum = keep.tile([P, TOKEN_TILES], F32)
+        inv_sum = keep.tile([P, TOKEN_TILES], F32)
+        e_out = keep.tile([P, TOKEN_TILES, SLOTS], F32)
+        w_out = keep.tile([P, TOKEN_TILES, SLOTS], F32)
+
+        nc.vector.memset(warm[:], 0.0)
+        nc.scalar.activation(out=warm[:, 1:2], in_=warm[:, 0:1], func=ACT.Exp)
+        make_identity(nc, ident[:])
+        nc.vector.memset(ones[:], 1.0)
+        nc.vector.memset(minus_half[:], -0.5)
+        nc.vector.memset(bias_rows[:], 0.0)
+
+        def load_weights(g):
+            nc.sync.dma_start(
+                out=w_raw[:, g].rearrange("p (u e) c -> p u e c", u=2),
+                in_=Wk[K_PASS * g : K_PASS * (g + 1), :].rearrange("(u p e) c -> p u e c", u=2, e=2),
+            )
+
+        def load_memory(c):
+            nc.sync.dma_start(
+                out=mem_sb[:, TILES_PER_CHUNK * c : TILES_PER_CHUNK * (c + 1), :],
+                in_=memory[N_PASS * c : N_PASS * (c + 1), :].rearrange("(n p) m -> p n m", p=P),
+            )
+
+        nc.sync.dma_start(out=bias_rows[0:1, :], in_=bk.unsqueeze(0))
+        load_weights(0)
+        load_memory(0)
+        load_weights(1)
+        for i in range(TOKEN_TILES):
+            nc.sync.dma_start(out=x_sb[:, i, :], in_=x_rows[P * i : P * (i + 1), :])
+        for c in range(1, CHUNKS):
+            load_memory(c)
+
+        bias_ps = psum.tile([P, D_KEY], F32, tag="bank")
+        nc.tensor.matmul(bias_ps[:], lhsT=ones[:], rhs=bias_rows[:], start=True, stop=True)
+        nc.scalar.mul(out=neg_bias[:], in_=bias_ps[:], mul=-1.0)
+
+        def weights_quantise(g):
+            nc.vector.tensor_copy(
+                out=w_grouped[:, g].rearrange("p (c i) t -> p c t i", i=4),
+                in_=w_raw[:, g].rearrange("p t (c i) -> p c t i", i=4),
+            )
+            nc.vector.quantize_mx(
+                out=w_codes[:, g, :].bitcast(FP8X4),
+                scales=w_scales[:, g, :],
+                in_=w_grouped[:, g].rearrange("p c t -> p (c t)"),
+            )
+
+        def tokens_quantise(i):
+            x_words = x_sb[:, i, :].bitcast(F32)
+            x_t = psum.tile([P, X_PASSES, 2, P], F32, tag="bank")
+            for g in range(X_PASSES):
+                for u in range(2):
+                    first = 256 * g + P * u
+                    nc.tensor.transpose(x_t[:, g, u, :], x_words[:, first : first + P], ident[:])
+            nc.scalar.copy(out=x_grouped[:, i], in_=x_t[:].rearrange("p g u r -> p g r u"))
+            nc.vector.quantize_mx(
+                out=x_codes[:, i, :].bitcast(FP8X4),
+                scales=x_scales[:, i, :],
+                in_=x_grouped[:, i].rearrange("p g r u -> p (g r u)").bitcast(BF16),
+            )
+
+        def memory_lengths(c):
+            first_tile = TILES_PER_CHUNK * c
+            tiles = slice(first_tile, first_tile + TILES_PER_CHUNK)
+            for n in range(first_tile, first_tile + TILES_PER_CHUNK):
+                m_squares = junk.tile([P, D_KEY], BF16)
+                nc.scalar.activation(
+                    out=m_squares[:], in_=mem_sb[:, n, :], func=ACT.Square, accum_out=m_sumsq[:, n : n + 1]
+                )
+            nc.gpsimd.tensor_scalar(out=m_floor[:, tiles], in0=m_sumsq[:, tiles], scalar1=EPS, scalar2=None, op0=ALU.max)
+            nc.gpsimd.tensor_tensor(out=m_rnorm[:, tiles], in0=m_floor[:, tiles], in1=minus_half[:], op=ALU.pow)
+
+        def memory_scale(c):
+            first_tile = TILES_PER_CHUNK * c
+            for n in range(first_tile, first_tile + TILES_PER_CHUNK):
+                nc.vector.tensor_scalar(
+                    out=mn[:, n, :], in0=mem_sb[:, n, :], scalar1=m_rnorm[:, n : n + 1], scalar2=None, op0=ALU.mult
+                )
+
+        def memory_transpose(c):
+            banks = []
+            first_tile = TILES_PER_CHUNK * c
+            for pair in range(first_tile, first_tile + TILES_PER_CHUNK, 2):
+                m_t = psum.tile([P, 2, 2, P], F32, tag="bank")
+                for j in range(2):
+                    mn_words = mn[:, pair + j, :].bitcast(F32)
+                    for u in range(2):
+                        nc.tensor.transpose(m_t[:, j, u, :], mn_words[:, P * u : P * (u + 1)], ident[:])
+                banks.append((pair, m_t))
+            return banks
+
+        def memory_regroup(banks):
+            for pair, m_t in banks:
+                nc.vector.tensor_copy(
+                    out=m_grouped[:, P * pair : P * (pair + 2), :].rearrange("p (j r) u -> p j r u", j=2),
+                    in_=m_t[:].rearrange("p j u r -> p j r u"),
+                )
+
+        def memory_quantise(c):
+            slots = slice(N_PASS * c, N_PASS * (c + 1))
+            nc.vector.quantize_mx(
+                out=m_codes[:, slots].bitcast(FP8X4),
+                scales=m_scales[:, slots],
+                in_=m_grouped[:, slots, :].rearrange("p s u -> p (s u)").bitcast(BF16),
+            )
+
+        def key_matmul(i):
+            z_ps = psum.tile([P, D_KEY], F32, tag="bank")
+            for g in range(X_PASSES):
+                nc.tensor.matmul_mx(
+                    out=z_ps[:],
+                    lhsT=x_codes[:, i, P * g : P * (g + 1)].bitcast(FP8X4),
+                    lhsT_scale=x_scales[:, i, P * g : P * (g + 1)],
+                    rhs=w_codes[:, g, :].bitcast(FP8X4),
+                    rhs_scale=w_scales[:, g, :],
+                    start=(g == 0),
+                    stop=(g == X_PASSES - 1),
+                )
+            return z_ps
+
+        def key_shift(i, z_ps):
+            nc.vector.tensor_tensor(out=neg_z[:, i, :], in0=neg_bias[:], in1=z_ps[:], op=ALU.subtract)
+            nc.vector.tensor_reduce(out=neg_z_min[:, i : i + 1], in_=neg_z[:, i, :], axis=AXIS_X, op=ALU.min)
+
+        def key_exp(i):
+            nc.scalar.activation(
+                out=e_key[:, i, :], in_=neg_z[:, i, :], func=ACT.Exp, bias=neg_z_min[:, i : i + 1], scale=-1.0
+            )
+            e_squares = junk.tile([P, D_KEY], F32)
+            nc.scalar.activation(out=e_squares[:], in_=e_key[:, i, :], func=ACT.Square, accum_out=k_sumsq[:, i : i + 1])
+            nc.gpsimd.tensor_tensor(
+                out=k_rnorm[:, i : i + 1], in0=k_sumsq[:, i : i + 1], in1=minus_half[:, 0:1], op=ALU.pow
+            )
+
+        def key_scale(i):
+            nc.vector.tensor_scalar(
+                out=kn[:, i, :], in0=e_key[:, i, :], scalar1=k_rnorm[:, i : i + 1], scalar2=None, op0=ALU.mult
+            )
+
+        def key_transpose(i):
+            kn_words = kn[:, i, :].bitcast(F32)
+            k_t = psum.tile([P, 2, P], F32, tag="bank")
+            for u in range(2):
+                nc.tensor.transpose(k_t[:, u, :], kn_words[:, P * u : P * (u + 1)], ident[:])
+            return k_t
+
+        def key_regroup(i, k_t):
+            nc.vector.tensor_copy(out=k_grouped[:, i], in_=k_t[:].rearrange("p u r -> p r u"))
+
+        def key_quantise(i):
+            nc.vector.quantize_mx(
+                out=k_codes[:, i, :].bitcast(FP8X4),
+                scales=k_scales[:, i, :],
+                in_=k_grouped[:, i].rearrange("p r u -> p (r u)").bitcast(BF16),
+            )
+
+        def similarities(i):
+            sims = []
+            for c in range(CHUNKS):
+                sims_ps = psum.tile([P, N_PASS], F32, tag="bank")
+                nc.tensor.matmul_mx(
+                    out=sims_ps[:],
+                    lhsT=k_codes[:, i, :].bitcast(FP8X4),
+                    lhsT_scale=k_scales[:, i, :],
+                    rhs=m_codes[:, N_PASS * c : N_PASS * (c + 1)].bitcast(FP8X4),
+                    rhs_scale=m_scales[:, N_PASS * c : N_PASS * (c + 1)],
+                    start=True,
+                    stop=True,
+                )
+                nc.vector.tensor_reduce(out=bank_min[:, i, c : c + 1], in_=sims_ps[:], axis=AXIS_X, op=ALU.min)
+                sims.append(sims_ps)
+            nc.vector.tensor_reduce(out=sims_min[:, i : i + 1], in_=bank_min[:, i, :], axis=AXIS_X, op=ALU.min)
+            return sims
+
+        def exponentials(i, sims):
+            for c in range(CHUNKS):
+                nc.scalar.activation(
+                    out=e_out[:, i, N_PASS * c : N_PASS * (c + 1)],
+                    in_=sims[c][:],
+                    func=ACT.Exp,
+                    bias=sims_min[:, i : i + 1],
+                    scale=-1.0,
+                    accum_out=bank_sum[:, i, c : c + 1],
+                )
+
+        def divide_and_store(i):
+            rows = out_rows[P * i : P * (i + 1), :]
+            nc.vector.tensor_reduce(out=row_sum[:, i : i + 1], in_=bank_sum[:, i, :], axis=AXIS_X, op=ALU.add)
+            nc.vector.reciprocal(out=inv_sum[:, i : i + 1], in_=row_sum[:, i : i + 1])
+            nc.vector.tensor_scalar(
+                out=w_out[:, i, :HALF], in0=e_out[:, i, :HALF], scalar1=inv_sum[:, i : i + 1], scalar2=None, op0=ALU.mult
+            )
+            nc.sync.dma_start(out=rows[:, :HALF], in_=w_out[:, i, :HALF])
+            nc.gpsimd.tensor_scalar(
+                out=w_out[:, i, HALF:],
+                in0=e_out[:, i, HALF:],
+                scalar1=inv_sum[:, i : i + 1],
+                scalar2=0.0,
+                op0=ALU.mult,
+                op1=ALU.add,
+            )
+            nc.sync.dma_start(out=rows[:, HALF:], in_=w_out[:, i, HALF:])
+
+        for g in range(X_PASSES):
+            weights_quantise(g)
+        memory_lengths(0)
+        for i in range(TOKEN_TILES):
+            tokens_quantise(i)
+        logits = [key_matmul(i) for i in range(TOKEN_TILES)]
+        memory_scale(0)
+        banks = memory_transpose(0)
+        for i in range(TOKEN_TILES):
+            key_shift(i, logits[i])
+        for c in range(1, CHUNKS):
+            memory_lengths(c)
+        for i in range(TOKEN_TILES):
+            key_exp(i)
+        for c in range(1, CHUNKS):
+            memory_scale(c)
+            next_banks = memory_transpose(c)
+            memory_regroup(banks)
+            memory_quantise(c - 1)
+            banks = next_banks
+        for i in range(TOKEN_TILES):
+            key_scale(i)
+        keys_t = [key_transpose(i) for i in range(TOKEN_TILES)]
+        memory_regroup(banks)
+        memory_quantise(CHUNKS - 1)
+        for i in range(TOKEN_TILES):
+            key_regroup(i, keys_t[i])
+        for i in range(TOKEN_TILES):
+            key_quantise(i)
+
+        sims = similarities(0)
+        for i in range(TOKEN_TILES):
+            exponentials(i, sims)
+            if i + 1 < TOKEN_TILES:
+                sims = similarities(i + 1)
+            divide_and_store(i)

@@ -22,7 +22,6 @@ X_PASSES = D_IN // K_PASS
 SLOT_TILES = SLOTS // P
 CHUNKS = SLOTS // N_PASS
 TILES_PER_CHUNK = N_PASS // P
-HALF = SLOTS // 2
 EPS = 1e-12
 
 FLOPS = 2 * TOKENS * D_IN * D_KEY + 2 * TOKENS * D_KEY * SLOTS
@@ -39,6 +38,7 @@ def tile_contentaddressablewritehead_pa_kernel(tc, controller_output, Wk, bk, me
 
         warm = keep.tile([P, 2], F32)
         ident = keep.tile([P, P], F32)
+        minus_one = keep.tile([P, 1], F32)
         ones = keep.tile([P, P], BF16)
         minus_half = keep.tile([P, TILES_PER_CHUNK], F32)
         bias_rows = keep.tile([P, D_KEY], BF16)
@@ -76,6 +76,9 @@ def tile_contentaddressablewritehead_pa_kernel(tc, controller_output, Wk, bk, me
         bank_min = keep.tile([P, TOKEN_TILES, CHUNKS], F32)
         sims_min = keep.tile([P, TOKEN_TILES], F32)
         bank_sum = keep.tile([P, TOKEN_TILES, CHUNKS], F32)
+        bank_factor = keep.tile([P, TOKEN_TILES, CHUNKS], F32)
+        bank_part = keep.tile([P, TOKEN_TILES, CHUNKS], F32)
+        half_sum = keep.tile([P, TOKEN_TILES, 2], F32)
         row_sum = keep.tile([P, TOKEN_TILES], F32)
         inv_sum = keep.tile([P, TOKEN_TILES], F32)
         e_out = keep.tile([P, TOKEN_TILES, SLOTS], F32)
@@ -83,10 +86,11 @@ def tile_contentaddressablewritehead_pa_kernel(tc, controller_output, Wk, bk, me
 
         nc.vector.memset(warm[:], 0.0)
         nc.scalar.activation(out=warm[:, 1:2], in_=warm[:, 0:1], func=ACT.Exp)
-        make_identity(nc, ident[:])
-        nc.vector.memset(ones[:], 1.0)
-        nc.vector.memset(minus_half[:], -0.5)
         nc.vector.memset(bias_rows[:], 0.0)
+        nc.vector.memset(ones[:], 1.0)
+        make_identity(nc, ident[:])
+        nc.gpsimd.memset(minus_half[:], -0.5)
+        nc.gpsimd.memset(minus_one[:], -1.0)
 
         def load_weights(g):
             nc.sync.dma_start(
@@ -94,86 +98,89 @@ def tile_contentaddressablewritehead_pa_kernel(tc, controller_output, Wk, bk, me
                 in_=Wk[K_PASS * g : K_PASS * (g + 1), :].rearrange("(u p e) c -> p u e c", u=2, e=2),
             )
 
-        def load_memory(c):
+        def load_memory(first, tiles):
             nc.sync.dma_start(
-                out=mem_sb[:, TILES_PER_CHUNK * c : TILES_PER_CHUNK * (c + 1), :],
-                in_=memory[N_PASS * c : N_PASS * (c + 1), :].rearrange("(n p) m -> p n m", p=P),
+                out=mem_sb[:, first : first + tiles, :],
+                in_=memory[P * first : P * (first + tiles), :].rearrange("(n p) m -> p n m", p=P),
             )
+
+        def load_tokens(i):
+            nc.sync.dma_start(out=x_sb[:, i, :], in_=x_rows[P * i : P * (i + 1), :])
 
         nc.sync.dma_start(out=bias_rows[0:1, :], in_=bk.unsqueeze(0))
         load_weights(0)
-        load_memory(0)
+        load_memory(0, 4)
         load_weights(1)
         for i in range(TOKEN_TILES):
-            nc.sync.dma_start(out=x_sb[:, i, :], in_=x_rows[P * i : P * (i + 1), :])
+            load_tokens(i)
         for c in range(1, CHUNKS):
-            load_memory(c)
+            load_memory(TILES_PER_CHUNK * c, TILES_PER_CHUNK)
 
         bias_ps = psum.tile([P, D_KEY], F32, tag="bank")
         nc.tensor.matmul(bias_ps[:], lhsT=ones[:], rhs=bias_rows[:], start=True, stop=True)
         nc.scalar.mul(out=neg_bias[:], in_=bias_ps[:], mul=-1.0)
 
-        def weights_quantise(g):
+        def weights_group(g):
             nc.vector.tensor_copy(
                 out=w_grouped[:, g].rearrange("p (c i) t -> p c t i", i=4),
                 in_=w_raw[:, g].rearrange("p t (c i) -> p c t i", i=4),
             )
+
+        def weights_quantise(g):
             nc.vector.quantize_mx(
                 out=w_codes[:, g, :].bitcast(FP8X4),
                 scales=w_scales[:, g, :],
                 in_=w_grouped[:, g].rearrange("p c t -> p (c t)"),
             )
 
-        def tokens_quantise(i):
+        def tokens_transpose(i):
             x_words = x_sb[:, i, :].bitcast(F32)
             x_t = psum.tile([P, X_PASSES, 2, P], F32, tag="bank")
             for g in range(X_PASSES):
                 for u in range(2):
                     first = 256 * g + P * u
                     nc.tensor.transpose(x_t[:, g, u, :], x_words[:, first : first + P], ident[:])
+            return x_t
+
+        def tokens_regroup(i, x_t):
             nc.scalar.copy(out=x_grouped[:, i], in_=x_t[:].rearrange("p g u r -> p g r u"))
+
+        def tokens_quantise(i):
             nc.vector.quantize_mx(
                 out=x_codes[:, i, :].bitcast(FP8X4),
                 scales=x_scales[:, i, :],
                 in_=x_grouped[:, i].rearrange("p g r u -> p (g r u)").bitcast(BF16),
             )
 
-        def memory_lengths(c):
-            first_tile = TILES_PER_CHUNK * c
-            tiles = slice(first_tile, first_tile + TILES_PER_CHUNK)
-            for n in range(first_tile, first_tile + TILES_PER_CHUNK):
+        def memory_lengths(pair):
+            tiles = slice(2 * pair, 2 * pair + 2)
+            for n in range(2 * pair, 2 * pair + 2):
                 m_squares = junk.tile([P, D_KEY], BF16)
                 nc.scalar.activation(
                     out=m_squares[:], in_=mem_sb[:, n, :], func=ACT.Square, accum_out=m_sumsq[:, n : n + 1]
                 )
             nc.gpsimd.tensor_scalar(out=m_floor[:, tiles], in0=m_sumsq[:, tiles], scalar1=EPS, scalar2=None, op0=ALU.max)
-            nc.gpsimd.tensor_tensor(out=m_rnorm[:, tiles], in0=m_floor[:, tiles], in1=minus_half[:], op=ALU.pow)
+            nc.gpsimd.tensor_tensor(out=m_rnorm[:, tiles], in0=m_floor[:, tiles], in1=minus_half[:, 0:2], op=ALU.pow)
 
-        def memory_scale(c):
-            first_tile = TILES_PER_CHUNK * c
-            for n in range(first_tile, first_tile + TILES_PER_CHUNK):
+        def memory_scale(pair):
+            for n in range(2 * pair, 2 * pair + 2):
                 nc.vector.tensor_scalar(
                     out=mn[:, n, :], in0=mem_sb[:, n, :], scalar1=m_rnorm[:, n : n + 1], scalar2=None, op0=ALU.mult
                 )
 
-        def memory_transpose(c):
-            banks = []
-            first_tile = TILES_PER_CHUNK * c
-            for pair in range(first_tile, first_tile + TILES_PER_CHUNK, 2):
-                m_t = psum.tile([P, 2, 2, P], F32, tag="bank")
-                for j in range(2):
-                    mn_words = mn[:, pair + j, :].bitcast(F32)
-                    for u in range(2):
-                        nc.tensor.transpose(m_t[:, j, u, :], mn_words[:, P * u : P * (u + 1)], ident[:])
-                banks.append((pair, m_t))
-            return banks
+        def memory_transpose(pair):
+            m_t = psum.tile([P, 2, 2, P], F32, tag="bank")
+            for j in range(2):
+                mn_words = mn[:, 2 * pair + j, :].bitcast(F32)
+                for u in range(2):
+                    nc.tensor.transpose(m_t[:, j, u, :], mn_words[:, P * u : P * (u + 1)], ident[:])
+            return m_t
 
-        def memory_regroup(banks):
-            for pair, m_t in banks:
-                nc.vector.tensor_copy(
-                    out=m_grouped[:, P * pair : P * (pair + 2), :].rearrange("p (j r) u -> p j r u", j=2),
-                    in_=m_t[:].rearrange("p j u r -> p j r u"),
-                )
+        def memory_regroup(copy, pair, m_t):
+            copy(
+                out=m_grouped[:, 2 * P * pair : 2 * P * (pair + 1), :].rearrange("p (j r) u -> p j r u", j=2),
+                in_=m_t[:].rearrange("p j u r -> p j r u"),
+            )
 
         def memory_quantise(c):
             slots = slice(N_PASS * c, N_PASS * (c + 1))
@@ -199,22 +206,26 @@ def tile_contentaddressablewritehead_pa_kernel(tc, controller_output, Wk, bk, me
 
         def key_shift(i, z_ps):
             nc.vector.tensor_tensor(out=neg_z[:, i, :], in0=neg_bias[:], in1=z_ps[:], op=ALU.subtract)
+
+        def key_min(i):
             nc.vector.tensor_reduce(out=neg_z_min[:, i : i + 1], in_=neg_z[:, i, :], axis=AXIS_X, op=ALU.min)
 
         def key_exp(i):
             nc.scalar.activation(
                 out=e_key[:, i, :], in_=neg_z[:, i, :], func=ACT.Exp, bias=neg_z_min[:, i : i + 1], scale=-1.0
             )
+
+        def key_length(i):
             e_squares = junk.tile([P, D_KEY], F32)
             nc.scalar.activation(out=e_squares[:], in_=e_key[:, i, :], func=ACT.Square, accum_out=k_sumsq[:, i : i + 1])
+
+        def key_rnorm(i):
             nc.gpsimd.tensor_tensor(
                 out=k_rnorm[:, i : i + 1], in0=k_sumsq[:, i : i + 1], in1=minus_half[:, 0:1], op=ALU.pow
             )
 
         def key_scale(i):
-            nc.vector.tensor_scalar(
-                out=kn[:, i, :], in0=e_key[:, i, :], scalar1=k_rnorm[:, i : i + 1], scalar2=None, op0=ALU.mult
-            )
+            nc.scalar.activation(out=kn[:, i, :], in_=e_key[:, i, :], func=ACT.Copy, scale=k_rnorm[:, i : i + 1])
 
         def key_transpose(i):
             kn_words = kn[:, i, :].bitcast(F32)
@@ -223,8 +234,8 @@ def tile_contentaddressablewritehead_pa_kernel(tc, controller_output, Wk, bk, me
                 nc.tensor.transpose(k_t[:, u, :], kn_words[:, P * u : P * (u + 1)], ident[:])
             return k_t
 
-        def key_regroup(i, k_t):
-            nc.vector.tensor_copy(out=k_grouped[:, i], in_=k_t[:].rearrange("p u r -> p r u"))
+        def key_regroup(copy, i, k_t):
+            copy(out=k_grouped[:, i], in_=k_t[:].rearrange("p u r -> p r u"))
 
         def key_quantise(i):
             nc.vector.quantize_mx(
@@ -233,86 +244,123 @@ def tile_contentaddressablewritehead_pa_kernel(tc, controller_output, Wk, bk, me
                 in_=k_grouped[:, i].rearrange("p r u -> p (r u)").bitcast(BF16),
             )
 
-        def similarities(i):
-            sims = []
-            for c in range(CHUNKS):
-                sims_ps = psum.tile([P, N_PASS], F32, tag="bank")
-                nc.tensor.matmul_mx(
-                    out=sims_ps[:],
-                    lhsT=k_codes[:, i, :].bitcast(FP8X4),
-                    lhsT_scale=k_scales[:, i, :],
-                    rhs=m_codes[:, N_PASS * c : N_PASS * (c + 1)].bitcast(FP8X4),
-                    rhs_scale=m_scales[:, N_PASS * c : N_PASS * (c + 1)],
-                    start=True,
-                    stop=True,
-                )
-                nc.vector.tensor_reduce(out=bank_min[:, i, c : c + 1], in_=sims_ps[:], axis=AXIS_X, op=ALU.min)
-                sims.append(sims_ps)
+        def similarity(i, c):
+            sims_ps = psum.tile([P, N_PASS], F32, tag="bank")
+            nc.tensor.matmul_mx(
+                out=sims_ps[:],
+                lhsT=k_codes[:, i, :].bitcast(FP8X4),
+                lhsT_scale=k_scales[:, i, :],
+                rhs=m_codes[:, N_PASS * c : N_PASS * (c + 1)].bitcast(FP8X4),
+                rhs_scale=m_scales[:, N_PASS * c : N_PASS * (c + 1)],
+                start=True,
+                stop=True,
+            )
+            return sims_ps
+
+        def minimum(i, c, sims_ps):
+            nc.vector.tensor_reduce(out=bank_min[:, i, c : c + 1], in_=sims_ps[:], axis=AXIS_X, op=ALU.min)
+
+        def exponential(i, c, sims_ps):
+            nc.scalar.activation(
+                out=e_out[:, i, N_PASS * c : N_PASS * (c + 1)],
+                in_=sims_ps[:],
+                func=ACT.Exp,
+                bias=bank_min[:, i, c : c + 1],
+                scale=-1.0,
+                accum_out=bank_sum[:, i, c : c + 1],
+            )
+
+        def row_min(i):
             nc.vector.tensor_reduce(out=sims_min[:, i : i + 1], in_=bank_min[:, i, :], axis=AXIS_X, op=ALU.min)
-            return sims
 
-        def exponentials(i, sims):
-            for c in range(CHUNKS):
-                nc.scalar.activation(
-                    out=e_out[:, i, N_PASS * c : N_PASS * (c + 1)],
-                    in_=sims[c][:],
-                    func=ACT.Exp,
-                    bias=sims_min[:, i : i + 1],
-                    scale=-1.0,
-                    accum_out=bank_sum[:, i, c : c + 1],
-                )
-
-        def divide_and_store(i):
-            rows = out_rows[P * i : P * (i + 1), :]
-            nc.vector.tensor_reduce(out=row_sum[:, i : i + 1], in_=bank_sum[:, i, :], axis=AXIS_X, op=ALU.add)
-            nc.vector.reciprocal(out=inv_sum[:, i : i + 1], in_=row_sum[:, i : i + 1])
-            nc.vector.tensor_scalar(
-                out=w_out[:, i, :HALF], in0=e_out[:, i, :HALF], scalar1=inv_sum[:, i : i + 1], scalar2=None, op0=ALU.mult
+        def join_factors(i):
+            nc.scalar.activation(
+                out=bank_factor[:, i, :], in_=bank_min[:, i, :], func=ACT.Exp, bias=sims_min[:, i : i + 1], scale=-1.0
             )
-            nc.sync.dma_start(out=rows[:, :HALF], in_=w_out[:, i, :HALF])
-            nc.gpsimd.tensor_scalar(
-                out=w_out[:, i, HALF:],
-                in0=e_out[:, i, HALF:],
-                scalar1=inv_sum[:, i : i + 1],
-                scalar2=0.0,
+
+        def join_gpsimd(i):
+            part = bank_part[:, i, :]
+            nc.gpsimd.tensor_tensor(out=part, in0=bank_sum[:, i, :], in1=bank_factor[:, i, :], op=ALU.mult)
+            nc.gpsimd.tensor_tensor(out=half_sum[:, i, :], in0=part[:, 0:2], in1=part[:, 2:4], op=ALU.add)
+            nc.gpsimd.tensor_tensor(
+                out=row_sum[:, i : i + 1], in0=half_sum[:, i, 0:1], in1=half_sum[:, i, 1:2], op=ALU.add
+            )
+            nc.gpsimd.tensor_tensor(out=inv_sum[:, i : i + 1], in0=row_sum[:, i : i + 1], in1=minus_one[:], op=ALU.pow)
+
+        def join_vector(i):
+            nc.vector.scalar_tensor_tensor(
+                out=bank_part[:, i, :],
+                in0=bank_sum[:, i, :],
+                scalar=1.0,
+                in1=bank_factor[:, i, :],
                 op0=ALU.mult,
-                op1=ALU.add,
+                op1=ALU.mult,
+                accum_out=row_sum[:, i : i + 1],
             )
-            nc.sync.dma_start(out=rows[:, HALF:], in_=w_out[:, i, HALF:])
+            nc.vector.reciprocal(out=inv_sum[:, i : i + 1], in_=row_sum[:, i : i + 1])
+
+        def divide(engine, i, c):
+            cols = slice(N_PASS * c, N_PASS * (c + 1))
+            engine.tensor_scalar(
+                out=w_out[:, i, cols],
+                in0=e_out[:, i, cols],
+                scalar1=bank_factor[:, i, c : c + 1],
+                scalar2=inv_sum[:, i : i + 1],
+                op0=ALU.mult,
+                op1=ALU.mult,
+            )
+            nc.sync.dma_start(out=out_rows[P * i : P * (i + 1), cols], in_=w_out[:, i, cols])
+
+        on_vector, on_scalar = nc.vector.tensor_copy, nc.scalar.copy
 
         for g in range(X_PASSES):
+            weights_group(g)
             weights_quantise(g)
-        memory_lengths(0)
+        for pair in range(2):
+            memory_lengths(pair)
         for i in range(TOKEN_TILES):
+            tokens_regroup(i, tokens_transpose(i))
             tokens_quantise(i)
         logits = [key_matmul(i) for i in range(TOKEN_TILES)]
-        memory_scale(0)
-        banks = memory_transpose(0)
+        for pair in range(2):
+            memory_scale(pair)
+        banks = [memory_transpose(pair) for pair in range(2)]
         for i in range(TOKEN_TILES):
             key_shift(i, logits[i])
-        for c in range(1, CHUNKS):
-            memory_lengths(c)
+            key_min(i)
+        for pair in range(2, 8):
+            memory_lengths(pair)
         for i in range(TOKEN_TILES):
             key_exp(i)
+            key_length(i)
+            key_rnorm(i)
         for c in range(1, CHUNKS):
-            memory_scale(c)
-            next_banks = memory_transpose(c)
-            memory_regroup(banks)
+            for pair in range(2 * c, 2 * c + 2):
+                memory_scale(pair)
+                banks.append(memory_transpose(pair))
+            for pair in range(2 * c - 2, 2 * c):
+                memory_regroup(on_vector, pair, banks[pair])
             memory_quantise(c - 1)
-            banks = next_banks
         for i in range(TOKEN_TILES):
             key_scale(i)
         keys_t = [key_transpose(i) for i in range(TOKEN_TILES)]
-        memory_regroup(banks)
+        for pair in range(6, 8):
+            memory_regroup(on_vector, pair, banks[pair])
         memory_quantise(CHUNKS - 1)
         for i in range(TOKEN_TILES):
-            key_regroup(i, keys_t[i])
+            key_regroup(on_vector, i, keys_t[i])
         for i in range(TOKEN_TILES):
             key_quantise(i)
 
-        sims = similarities(0)
         for i in range(TOKEN_TILES):
-            exponentials(i, sims)
-            if i + 1 < TOKEN_TILES:
-                sims = similarities(i + 1)
-            divide_and_store(i)
+            for c in range(CHUNKS):
+                sims_ps = similarity(i, c)
+                minimum(i, c, sims_ps)
+                exponential(i, c, sims_ps)
+            row_min(i)
+            join_factors(i)
+            join_vector(i)
+            divide(nc.vector, i, 0)
+            divide(nc.gpsimd, i, 2)
+            divide(nc.vector, i, 1)
+            divide(nc.gpsimd, i, 3)

@@ -108,13 +108,17 @@ def tile_contentaddressablewritehead_pa_kernel(tc, controller_output, Wk, bk, me
             nc.sync.dma_start(out=x_sb[:, i, :], in_=x_rows[P * i : P * (i + 1), :])
 
         nc.sync.dma_start(out=bias_rows[0:1, :], in_=bk.unsqueeze(0))
+        load_tokens(0)
+        load_memory(0, 2)
         load_weights(0)
-        load_memory(0, 4)
         load_weights(1)
-        for i in range(TOKEN_TILES):
-            load_tokens(i)
-        for c in range(1, CHUNKS):
-            load_memory(TILES_PER_CHUNK * c, TILES_PER_CHUNK)
+        load_tokens(1)
+        load_memory(2, 2)
+        load_tokens(2)
+        load_tokens(3)
+        load_memory(4, 4)
+        load_memory(8, 4)
+        load_memory(12, 4)
 
         bias_ps = psum.tile([P, D_KEY], F32, tag="bank")
         nc.tensor.matmul(bias_ps[:], lhsT=ones[:], rhs=bias_rows[:], start=True, stop=True)
@@ -225,7 +229,9 @@ def tile_contentaddressablewritehead_pa_kernel(tc, controller_output, Wk, bk, me
             )
 
         def key_scale(i):
-            nc.scalar.activation(out=kn[:, i, :], in_=e_key[:, i, :], func=ACT.Copy, scale=k_rnorm[:, i : i + 1])
+            nc.vector.tensor_scalar(
+                out=kn[:, i, :], in0=e_key[:, i, :], scalar1=k_rnorm[:, i : i + 1], scalar2=None, op0=ALU.mult
+            )
 
         def key_transpose(i):
             kn_words = kn[:, i, :].bitcast(F32)
@@ -339,16 +345,16 @@ def tile_contentaddressablewritehead_pa_kernel(tc, controller_output, Wk, bk, me
                 memory_scale(pair)
                 banks.append(memory_transpose(pair))
             for pair in range(2 * c - 2, 2 * c):
-                memory_regroup(on_vector, pair, banks[pair])
+                memory_regroup(on_scalar if pair in (6,7,) else on_vector, pair, banks[pair])
             memory_quantise(c - 1)
         for i in range(TOKEN_TILES):
             key_scale(i)
         keys_t = [key_transpose(i) for i in range(TOKEN_TILES)]
         for pair in range(6, 8):
-            memory_regroup(on_vector, pair, banks[pair])
+            memory_regroup(on_scalar if pair in (6,7,) else on_vector, pair, banks[pair])
         memory_quantise(CHUNKS - 1)
         for i in range(TOKEN_TILES):
-            key_regroup(on_vector, i, keys_t[i])
+            key_regroup(on_scalar if i in (0,1,2,3,) else on_vector, i, keys_t[i])
         for i in range(TOKEN_TILES):
             key_quantise(i)
 
@@ -360,7 +366,5 @@ def tile_contentaddressablewritehead_pa_kernel(tc, controller_output, Wk, bk, me
             row_min(i)
             join_factors(i)
             join_vector(i)
-            divide(nc.vector, i, 0)
-            divide(nc.gpsimd, i, 2)
-            divide(nc.vector, i, 1)
-            divide(nc.gpsimd, i, 3)
+            for c, e in [[[0,"V"],[2,"V"],[1,"V"],[3,"V"]],[[0,"V"],[2,"V"],[1,"V"],[3,"V"]],[[0,"V"],[2,"V"],[1,"V"],[3,"V"]],[[0,"V"],[2,"V"],[1,"V"],[3,"V"]]][i]:
+                divide(nc.vector if e == "V" else nc.gpsimd, i, c)

@@ -34,11 +34,10 @@ def tile_contentaddressablewritehead_pa_kernel(tc, controller_output, Wk, bk, me
 
     with tc.tile_pool(name="keep", bufs=1) as keep, tc.tile_pool(name="junk", bufs=4) as junk, tc.psum_pool(
         name="psum", bufs=8
-    ) as psum:
+    ) as psum, tc.manual_schedule():
 
         warm = keep.tile([P, 2], F32)
         ident = keep.tile([P, P], F32)
-        minus_one = keep.tile([P, 1], F32)
         ones = keep.tile([P, P], BF16)
         minus_half = keep.tile([P, TILES_PER_CHUNK], F32)
         bias_rows = keep.tile([P, D_KEY], BF16)
@@ -78,7 +77,6 @@ def tile_contentaddressablewritehead_pa_kernel(tc, controller_output, Wk, bk, me
         bank_sum = keep.tile([P, TOKEN_TILES, CHUNKS], F32)
         bank_factor = keep.tile([P, TOKEN_TILES, CHUNKS], F32)
         bank_part = keep.tile([P, TOKEN_TILES, CHUNKS], F32)
-        half_sum = keep.tile([P, TOKEN_TILES, 2], F32)
         row_sum = keep.tile([P, TOKEN_TILES], F32)
         inv_sum = keep.tile([P, TOKEN_TILES], F32)
         e_out = keep.tile([P, TOKEN_TILES, SLOTS], F32)
@@ -90,7 +88,6 @@ def tile_contentaddressablewritehead_pa_kernel(tc, controller_output, Wk, bk, me
         nc.vector.memset(ones[:], 1.0)
         make_identity(nc, ident[:])
         nc.gpsimd.memset(minus_half[:], -0.5)
-        nc.gpsimd.memset(minus_one[:], -1.0)
 
         def load_weights(g):
             nc.sync.dma_start(
@@ -108,9 +105,9 @@ def tile_contentaddressablewritehead_pa_kernel(tc, controller_output, Wk, bk, me
             nc.sync.dma_start(out=x_sb[:, i, :], in_=x_rows[P * i : P * (i + 1), :])
 
         nc.sync.dma_start(out=bias_rows[0:1, :], in_=bk.unsqueeze(0))
-        load_tokens(0)
         load_memory(0, 2)
         load_weights(0)
+        load_tokens(0)
         load_weights(1)
         load_tokens(1)
         load_memory(2, 2)
@@ -284,16 +281,7 @@ def tile_contentaddressablewritehead_pa_kernel(tc, controller_output, Wk, bk, me
                 out=bank_factor[:, i, :], in_=bank_min[:, i, :], func=ACT.Exp, bias=sims_min[:, i : i + 1], scale=-1.0
             )
 
-        def join_gpsimd(i):
-            part = bank_part[:, i, :]
-            nc.gpsimd.tensor_tensor(out=part, in0=bank_sum[:, i, :], in1=bank_factor[:, i, :], op=ALU.mult)
-            nc.gpsimd.tensor_tensor(out=half_sum[:, i, :], in0=part[:, 0:2], in1=part[:, 2:4], op=ALU.add)
-            nc.gpsimd.tensor_tensor(
-                out=row_sum[:, i : i + 1], in0=half_sum[:, i, 0:1], in1=half_sum[:, i, 1:2], op=ALU.add
-            )
-            nc.gpsimd.tensor_tensor(out=inv_sum[:, i : i + 1], in0=row_sum[:, i : i + 1], in1=minus_one[:], op=ALU.pow)
-
-        def join_vector(i):
+        def join_sum(i):
             nc.vector.scalar_tensor_tensor(
                 out=bank_part[:, i, :],
                 in0=bank_sum[:, i, :],
@@ -303,6 +291,8 @@ def tile_contentaddressablewritehead_pa_kernel(tc, controller_output, Wk, bk, me
                 op1=ALU.mult,
                 accum_out=row_sum[:, i : i + 1],
             )
+
+        def join_inverse(i):
             nc.vector.reciprocal(out=inv_sum[:, i : i + 1], in_=row_sum[:, i : i + 1])
 
         def divide(engine, i, c):
@@ -319,52 +309,175 @@ def tile_contentaddressablewritehead_pa_kernel(tc, controller_output, Wk, bk, me
 
         on_vector, on_scalar = nc.vector.tensor_copy, nc.scalar.copy
 
-        for g in range(X_PASSES):
-            weights_group(g)
-            weights_quantise(g)
-        for pair in range(2):
-            memory_lengths(pair)
-        for i in range(TOKEN_TILES):
-            tokens_regroup(i, tokens_transpose(i))
-            tokens_quantise(i)
-        logits = [key_matmul(i) for i in range(TOKEN_TILES)]
-        for pair in range(2):
-            memory_scale(pair)
-        banks = [memory_transpose(pair) for pair in range(2)]
-        for i in range(TOKEN_TILES):
-            key_shift(i, logits[i])
-            key_min(i)
-        for pair in range(2, 8):
-            memory_lengths(pair)
-        for i in range(TOKEN_TILES):
-            key_exp(i)
-            key_length(i)
-            key_rnorm(i)
-        for c in range(1, CHUNKS):
-            for pair in range(2 * c, 2 * c + 2):
-                memory_scale(pair)
-                banks.append(memory_transpose(pair))
-            for pair in range(2 * c - 2, 2 * c):
-                memory_regroup(on_scalar if pair in (6,7,) else on_vector, pair, banks[pair])
-            memory_quantise(c - 1)
-        for i in range(TOKEN_TILES):
-            key_scale(i)
-        keys_t = [key_transpose(i) for i in range(TOKEN_TILES)]
-        for pair in range(6, 8):
-            memory_regroup(on_scalar if pair in (6,7,) else on_vector, pair, banks[pair])
-        memory_quantise(CHUNKS - 1)
-        for i in range(TOKEN_TILES):
-            key_regroup(on_scalar if i in (0,1,2,3,) else on_vector, i, keys_t[i])
-        for i in range(TOKEN_TILES):
-            key_quantise(i)
-
-        for i in range(TOKEN_TILES):
-            for c in range(CHUNKS):
-                sims_ps = similarity(i, c)
-                minimum(i, c, sims_ps)
-                exponential(i, c, sims_ps)
-            row_min(i)
-            join_factors(i)
-            join_vector(i)
-            for c, e in [[[0,"V"],[2,"V"],[1,"V"],[3,"V"]],[[0,"V"],[2,"V"],[1,"V"],[3,"V"]],[[0,"V"],[2,"V"],[1,"V"],[3,"V"]],[[0,"V"],[2,"V"],[1,"V"],[3,"V"]]][i]:
-                divide(nc.vector if e == "V" else nc.gpsimd, i, c)
+        x0 = tokens_transpose(0)
+        x1 = tokens_transpose(1)
+        x2 = tokens_transpose(2)
+        x3 = tokens_transpose(3)
+        weights_group(0)
+        memory_lengths(0)
+        weights_group(1)
+        tokens_regroup(0, x0)
+        weights_quantise(0)
+        memory_lengths(1)
+        weights_quantise(1)
+        tokens_regroup(1, x1)
+        tokens_quantise(0)
+        tokens_regroup(2, x2)
+        z0 = key_matmul(0)
+        memory_scale(0)
+        memory_lengths(2)
+        m0 = memory_transpose(0)
+        tokens_quantise(1)
+        tokens_regroup(3, x3)
+        z1 = key_matmul(1)
+        memory_scale(1)
+        memory_lengths(3)
+        tokens_quantise(2)
+        memory_lengths(4)
+        z2 = key_matmul(2)
+        m1 = memory_transpose(1)
+        key_shift(0, z0)
+        memory_lengths(5)
+        tokens_quantise(3)
+        memory_lengths(6)
+        z3 = key_matmul(3)
+        key_min(0)
+        memory_lengths(7)
+        key_shift(1, z1)
+        key_exp(0)
+        key_shift(2, z2)
+        key_min(1)
+        key_exp(1)
+        key_min(2)
+        key_length(0)
+        key_rnorm(0)
+        key_shift(3, z3)
+        key_length(1)
+        key_rnorm(1)
+        memory_scale(2)
+        key_exp(2)
+        m2 = memory_transpose(2)
+        key_min(3)
+        key_exp(3)
+        memory_scale(3)
+        key_length(2)
+        key_rnorm(2)
+        m3 = memory_transpose(3)
+        memory_regroup(on_vector, 0, m0)
+        key_length(3)
+        key_rnorm(3)
+        memory_regroup(on_vector, 1, m1)
+        memory_scale(4)
+        m4 = memory_transpose(4)
+        memory_quantise(0)
+        memory_scale(5)
+        m5 = memory_transpose(5)
+        memory_regroup(on_vector, 2, m2)
+        memory_regroup(on_vector, 3, m3)
+        memory_scale(6)
+        m6 = memory_transpose(6)
+        memory_quantise(1)
+        memory_regroup(on_scalar, 6, m6)
+        memory_scale(7)
+        m7 = memory_transpose(7)
+        memory_regroup(on_vector, 4, m4)
+        memory_regroup(on_scalar, 7, m7)
+        memory_regroup(on_vector, 5, m5)
+        key_scale(0)
+        k0 = key_transpose(0)
+        key_scale(1)
+        key_regroup(on_scalar, 0, k0)
+        k1 = key_transpose(1)
+        memory_quantise(2)
+        key_regroup(on_scalar, 1, k1)
+        key_scale(2)
+        k2 = key_transpose(2)
+        key_scale(3)
+        key_regroup(on_scalar, 2, k2)
+        k3 = key_transpose(3)
+        memory_quantise(3)
+        key_regroup(on_scalar, 3, k3)
+        key_quantise(0)
+        s00 = similarity(0, 0)
+        s01 = similarity(0, 1)
+        s02 = similarity(0, 2)
+        s03 = similarity(0, 3)
+        key_quantise(1)
+        s10 = similarity(1, 0)
+        s11 = similarity(1, 1)
+        s12 = similarity(1, 2)
+        s13 = similarity(1, 3)
+        key_quantise(2)
+        s20 = similarity(2, 0)
+        s21 = similarity(2, 1)
+        s22 = similarity(2, 2)
+        s23 = similarity(2, 3)
+        minimum(0, 0, s00)
+        exponential(0, 0, s00)
+        key_quantise(3)
+        s30 = similarity(3, 0)
+        s31 = similarity(3, 1)
+        s32 = similarity(3, 2)
+        s33 = similarity(3, 3)
+        minimum(0, 1, s01)
+        exponential(0, 1, s01)
+        minimum(0, 2, s02)
+        exponential(0, 2, s02)
+        minimum(0, 3, s03)
+        exponential(0, 3, s03)
+        minimum(1, 0, s10)
+        row_min(0)
+        join_factors(0)
+        minimum(1, 1, s11)
+        exponential(1, 0, s10)
+        minimum(1, 2, s12)
+        exponential(1, 1, s11)
+        join_sum(0)
+        exponential(1, 2, s12)
+        minimum(1, 3, s13)
+        exponential(1, 3, s13)
+        join_inverse(0)
+        divide(nc.gpsimd, 0, 0)
+        minimum(2, 0, s20)
+        divide(nc.gpsimd, 0, 1)
+        row_min(1)
+        join_factors(1)
+        divide(nc.gpsimd, 0, 2)
+        minimum(2, 1, s21)
+        exponential(2, 0, s20)
+        divide(nc.gpsimd, 0, 3)
+        minimum(2, 2, s22)
+        exponential(2, 1, s21)
+        join_sum(1)
+        exponential(2, 2, s22)
+        minimum(2, 3, s23)
+        exponential(2, 3, s23)
+        join_inverse(1)
+        minimum(3, 0, s30)
+        divide(nc.vector, 1, 0)
+        row_min(2)
+        join_factors(2)
+        divide(nc.vector, 1, 1)
+        exponential(3, 0, s30)
+        divide(nc.vector, 1, 2)
+        minimum(3, 1, s31)
+        exponential(3, 1, s31)
+        divide(nc.vector, 1, 3)
+        minimum(3, 2, s32)
+        exponential(3, 2, s32)
+        join_sum(2)
+        minimum(3, 3, s33)
+        exponential(3, 3, s33)
+        join_inverse(2)
+        row_min(3)
+        join_factors(3)
+        divide(nc.vector, 2, 0)
+        divide(nc.vector, 2, 1)
+        divide(nc.vector, 2, 2)
+        divide(nc.vector, 2, 3)
+        join_sum(3)
+        join_inverse(3)
+        divide(nc.vector, 3, 0)
+        divide(nc.vector, 3, 1)
+        divide(nc.vector, 3, 2)
+        divide(nc.vector, 3, 3)

@@ -104,9 +104,12 @@ def tile_contentaddressablewritehead_pa_kernel(tc, controller_output, Wk, bk, me
         def load_tokens(i):
             nc.sync.dma_start(out=x_sb[:, i, :], in_=x_rows[P * i : P * (i + 1), :])
 
-        nc.sync.dma_start(out=bias_rows[0:1, :], in_=bk.unsqueeze(0))
+        def load_bias():
+            nc.sync.dma_start(out=bias_rows[0:1, :], in_=bk.unsqueeze(0))
+
         load_memory(0, 2)
         load_weights(0)
+        load_bias()
         load_tokens(0)
         load_weights(1)
         load_tokens(1)
@@ -117,9 +120,13 @@ def tile_contentaddressablewritehead_pa_kernel(tc, controller_output, Wk, bk, me
         load_memory(8, 4)
         load_memory(12, 4)
 
-        bias_ps = psum.tile([P, D_KEY], F32, tag="bank")
-        nc.tensor.matmul(bias_ps[:], lhsT=ones[:], rhs=bias_rows[:], start=True, stop=True)
-        nc.scalar.mul(out=neg_bias[:], in_=bias_ps[:], mul=-1.0)
+        def bias_matmul():
+            bias_ps = psum.tile([P, D_KEY], F32, tag="bank")
+            nc.tensor.matmul(bias_ps[:], lhsT=ones[:], rhs=bias_rows[:], start=True, stop=True)
+            return bias_ps
+
+        def bias_negate(bias_ps):
+            nc.scalar.mul(out=neg_bias[:], in_=bias_ps[:], mul=-1.0)
 
         def weights_group(g):
             nc.vector.tensor_copy(
@@ -309,64 +316,66 @@ def tile_contentaddressablewritehead_pa_kernel(tc, controller_output, Wk, bk, me
 
         on_vector, on_scalar = nc.vector.tensor_copy, nc.scalar.copy
 
+        bias_ps = bias_matmul()
         x0 = tokens_transpose(0)
         x1 = tokens_transpose(1)
         x2 = tokens_transpose(2)
         x3 = tokens_transpose(3)
         weights_group(0)
         memory_lengths(0)
+        memory_scale(0)
+        bias_negate(bias_ps)
         weights_group(1)
         tokens_regroup(0, x0)
         weights_quantise(0)
         memory_lengths(1)
-        weights_quantise(1)
-        tokens_regroup(1, x1)
         tokens_quantise(0)
+        tokens_regroup(1, x1)
+        weights_quantise(1)
         tokens_regroup(2, x2)
         z0 = key_matmul(0)
-        memory_scale(0)
-        memory_lengths(2)
         m0 = memory_transpose(0)
         tokens_quantise(1)
-        tokens_regroup(3, x3)
+        memory_lengths(2)
         z1 = key_matmul(1)
         memory_scale(1)
-        memory_lengths(3)
+        tokens_regroup(3, x3)
         tokens_quantise(2)
-        memory_lengths(4)
+        memory_lengths(3)
         z2 = key_matmul(2)
         m1 = memory_transpose(1)
         key_shift(0, z0)
-        memory_lengths(5)
-        tokens_quantise(3)
-        memory_lengths(6)
-        z3 = key_matmul(3)
-        key_min(0)
-        memory_lengths(7)
+        memory_lengths(4)
         key_shift(1, z1)
+        memory_lengths(5)
+        key_min(0)
         key_exp(0)
-        key_shift(2, z2)
+        tokens_quantise(3)
+        z3 = key_matmul(3)
         key_min(1)
         key_exp(1)
-        key_min(2)
+        key_shift(2, z2)
         key_length(0)
         key_rnorm(0)
-        key_shift(3, z3)
+        memory_scale(2)
         key_length(1)
         key_rnorm(1)
-        memory_scale(2)
-        key_exp(2)
         m2 = memory_transpose(2)
+        key_min(2)
+        memory_lengths(6)
+        key_shift(3, z3)
+        memory_lengths(7)
+        memory_scale(3)
+        key_exp(2)
+        m3 = memory_transpose(3)
         key_min(3)
         key_exp(3)
-        memory_scale(3)
+        memory_regroup(on_vector, 0, m0)
         key_length(2)
         key_rnorm(2)
-        m3 = memory_transpose(3)
-        memory_regroup(on_vector, 0, m0)
+        memory_regroup(on_vector, 1, m1)
         key_length(3)
         key_rnorm(3)
-        memory_regroup(on_vector, 1, m1)
         memory_scale(4)
         m4 = memory_transpose(4)
         memory_quantise(0)
@@ -374,57 +383,57 @@ def tile_contentaddressablewritehead_pa_kernel(tc, controller_output, Wk, bk, me
         m5 = memory_transpose(5)
         memory_regroup(on_vector, 2, m2)
         memory_regroup(on_vector, 3, m3)
-        memory_scale(6)
-        m6 = memory_transpose(6)
-        memory_quantise(1)
-        memory_regroup(on_scalar, 6, m6)
-        memory_scale(7)
-        m7 = memory_transpose(7)
-        memory_regroup(on_vector, 4, m4)
-        memory_regroup(on_scalar, 7, m7)
-        memory_regroup(on_vector, 5, m5)
         key_scale(0)
         k0 = key_transpose(0)
         key_scale(1)
         key_regroup(on_scalar, 0, k0)
         k1 = key_transpose(1)
-        memory_quantise(2)
+        memory_quantise(1)
         key_regroup(on_scalar, 1, k1)
-        key_scale(2)
-        k2 = key_transpose(2)
-        key_scale(3)
-        key_regroup(on_scalar, 2, k2)
-        k3 = key_transpose(3)
-        memory_quantise(3)
-        key_regroup(on_scalar, 3, k3)
+        memory_scale(6)
+        m6 = memory_transpose(6)
+        memory_regroup(on_vector, 4, m4)
+        memory_regroup(on_scalar, 6, m6)
+        memory_scale(7)
+        m7 = memory_transpose(7)
+        memory_regroup(on_vector, 5, m5)
+        memory_regroup(on_scalar, 7, m7)
         key_quantise(0)
         s00 = similarity(0, 0)
         s01 = similarity(0, 1)
-        s02 = similarity(0, 2)
-        s03 = similarity(0, 3)
+        memory_quantise(2)
         key_quantise(1)
+        key_scale(2)
+        k2 = key_transpose(2)
+        s02 = similarity(0, 2)
+        minimum(0, 0, s00)
+        key_regroup(on_scalar, 2, k2)
+        key_scale(3)
+        k3 = key_transpose(3)
+        minimum(0, 1, s01)
+        key_regroup(on_scalar, 3, k3)
+        memory_quantise(3)
+        exponential(0, 0, s00)
+        s03 = similarity(0, 3)
         s10 = similarity(1, 0)
         s11 = similarity(1, 1)
         s12 = similarity(1, 2)
         s13 = similarity(1, 3)
+        minimum(0, 2, s02)
+        exponential(0, 1, s01)
         key_quantise(2)
+        exponential(0, 2, s02)
         s20 = similarity(2, 0)
         s21 = similarity(2, 1)
         s22 = similarity(2, 2)
         s23 = similarity(2, 3)
-        minimum(0, 0, s00)
-        exponential(0, 0, s00)
+        minimum(0, 3, s03)
+        exponential(0, 3, s03)
         key_quantise(3)
         s30 = similarity(3, 0)
         s31 = similarity(3, 1)
         s32 = similarity(3, 2)
         s33 = similarity(3, 3)
-        minimum(0, 1, s01)
-        exponential(0, 1, s01)
-        minimum(0, 2, s02)
-        exponential(0, 2, s02)
-        minimum(0, 3, s03)
-        exponential(0, 3, s03)
         minimum(1, 0, s10)
         row_min(0)
         join_factors(0)

@@ -96,10 +96,9 @@ def tile_contentaddressablewritehead_pa_kernel(tc, controller_output, Wk, bk, me
             )
 
         def load_memory(first, tiles):
-            nc.sync.dma_start(
-                out=mem_sb[:, first : first + tiles, :],
-                in_=memory[P * first : P * (first + tiles), :].rearrange("(n p) m -> p n m", p=P),
-            )
+            c, j = divmod(first, TILES_PER_CHUNK)
+            chunk = memory[N_PASS * c : N_PASS * (c + 1), :].rearrange("(p j) m -> p j m", j=TILES_PER_CHUNK)
+            nc.sync.dma_start(out=mem_sb[:, first : first + tiles, :], in_=chunk[:, j : j + tiles, :])
 
         def load_tokens(i):
             nc.sync.dma_start(out=x_sb[:, i, :], in_=x_rows[P * i : P * (i + 1), :])
@@ -185,10 +184,9 @@ def tile_contentaddressablewritehead_pa_kernel(tc, controller_output, Wk, bk, me
             return m_t
 
         def memory_regroup(copy, pair, m_t):
-            copy(
-                out=m_grouped[:, 2 * P * pair : 2 * P * (pair + 1), :].rearrange("p (j r) u -> p j r u", j=2),
-                in_=m_t[:].rearrange("p j u r -> p j r u"),
-            )
+            c, half = divmod(pair, 2)
+            slots = m_grouped[:, N_PASS * c : N_PASS * (c + 1), :].rearrange("p (r j) u -> p r j u", j=TILES_PER_CHUNK)
+            copy(out=slots[:, :, 2 * half : 2 * half + 2, :], in_=m_t[:].rearrange("p j u r -> p r j u"))
 
         def memory_quantise(c):
             slots = slice(N_PASS * c, N_PASS * (c + 1))
@@ -312,6 +310,9 @@ def tile_contentaddressablewritehead_pa_kernel(tc, controller_output, Wk, bk, me
                 op0=ALU.mult,
                 op1=ALU.mult,
             )
+
+        def store(i, c, banks=1):
+            cols = slice(N_PASS * c, N_PASS * (c + banks))
             nc.sync.dma_start(out=out_rows[P * i : P * (i + 1), cols], in_=w_out[:, i, cols])
 
         on_vector, on_scalar = nc.vector.tensor_copy, nc.scalar.copy
@@ -334,10 +335,10 @@ def tile_contentaddressablewritehead_pa_kernel(tc, controller_output, Wk, bk, me
         weights_quantise(1)
         tokens_regroup(2, x2)
         z0 = key_matmul(0)
-        m0 = memory_transpose(0)
         tokens_quantise(1)
         memory_lengths(2)
         z1 = key_matmul(1)
+        m0 = memory_transpose(0)
         memory_scale(1)
         tokens_regroup(3, x3)
         tokens_quantise(2)
@@ -407,22 +408,22 @@ def tile_contentaddressablewritehead_pa_kernel(tc, controller_output, Wk, bk, me
         k2 = key_transpose(2)
         s02 = similarity(0, 2)
         minimum(0, 0, s00)
-        key_regroup(on_scalar, 2, k2)
+        exponential(0, 0, s00)
         key_scale(3)
+        key_regroup(on_scalar, 2, k2)
         k3 = key_transpose(3)
         minimum(0, 1, s01)
-        key_regroup(on_scalar, 3, k3)
+        exponential(0, 1, s01)
         memory_quantise(3)
-        exponential(0, 0, s00)
+        key_regroup(on_scalar, 3, k3)
         s03 = similarity(0, 3)
         s10 = similarity(1, 0)
         s11 = similarity(1, 1)
         s12 = similarity(1, 2)
         s13 = similarity(1, 3)
         minimum(0, 2, s02)
-        exponential(0, 1, s01)
-        key_quantise(2)
         exponential(0, 2, s02)
+        key_quantise(2)
         s20 = similarity(2, 0)
         s21 = similarity(2, 1)
         s22 = similarity(2, 2)
@@ -449,12 +450,14 @@ def tile_contentaddressablewritehead_pa_kernel(tc, controller_output, Wk, bk, me
         divide(nc.gpsimd, 0, 0)
         minimum(2, 0, s20)
         divide(nc.gpsimd, 0, 1)
+        store(0, 0, banks=2)
         row_min(1)
         join_factors(1)
         divide(nc.gpsimd, 0, 2)
         minimum(2, 1, s21)
         exponential(2, 0, s20)
         divide(nc.gpsimd, 0, 3)
+        store(0, 2, banks=2)
         minimum(2, 2, s22)
         exponential(2, 1, s21)
         join_sum(1)
@@ -468,10 +471,12 @@ def tile_contentaddressablewritehead_pa_kernel(tc, controller_output, Wk, bk, me
         join_factors(2)
         divide(nc.vector, 1, 1)
         exponential(3, 0, s30)
+        store(1, 0, banks=2)
         divide(nc.vector, 1, 2)
         minimum(3, 1, s31)
         exponential(3, 1, s31)
         divide(nc.vector, 1, 3)
+        store(1, 2, banks=2)
         minimum(3, 2, s32)
         exponential(3, 2, s32)
         join_sum(2)
@@ -482,11 +487,17 @@ def tile_contentaddressablewritehead_pa_kernel(tc, controller_output, Wk, bk, me
         join_factors(3)
         divide(nc.vector, 2, 0)
         divide(nc.vector, 2, 1)
+        store(2, 0, banks=2)
         divide(nc.vector, 2, 2)
         divide(nc.vector, 2, 3)
+        store(2, 2, banks=2)
         join_sum(3)
         join_inverse(3)
         divide(nc.vector, 3, 0)
+        store(3, 0)
         divide(nc.vector, 3, 1)
+        store(3, 1)
         divide(nc.vector, 3, 2)
+        store(3, 2)
         divide(nc.vector, 3, 3)
+        store(3, 3)

@@ -448,49 +448,55 @@ def tile_contentaddressablewritehead_pa_kernel(tc, controller_output, Wk, bk, me
         exponential(1, 3, s13)
         join_inverse(0)
         divide(nc.gpsimd, 0, 0)
+        store(0, 0)
         minimum(2, 0, s20)
         divide(nc.gpsimd, 0, 1)
-        store(0, 0, banks=2)
+        store(0, 1)
         row_min(1)
         join_factors(1)
         divide(nc.gpsimd, 0, 2)
+        store(0, 2)
         minimum(2, 1, s21)
         exponential(2, 0, s20)
         divide(nc.gpsimd, 0, 3)
-        store(0, 2, banks=2)
+        store(0, 3)
         minimum(2, 2, s22)
         exponential(2, 1, s21)
-        join_sum(1)
-        exponential(2, 2, s22)
         minimum(2, 3, s23)
+        exponential(2, 2, s22)
+        join_sum(1)
         exponential(2, 3, s23)
-        join_inverse(1)
         minimum(3, 0, s30)
-        divide(nc.vector, 1, 0)
+        join_inverse(1)
         row_min(2)
         join_factors(2)
-        divide(nc.vector, 1, 1)
-        exponential(3, 0, s30)
-        store(1, 0, banks=2)
-        divide(nc.vector, 1, 2)
         minimum(3, 1, s31)
+        exponential(3, 0, s30)
+        divide(nc.vector, 1, 0)
         exponential(3, 1, s31)
-        divide(nc.vector, 1, 3)
-        store(1, 2, banks=2)
+        store(1, 0)
+        divide(nc.vector, 1, 1)
+        store(1, 1)
         minimum(3, 2, s32)
         exponential(3, 2, s32)
+        divide(nc.vector, 1, 2)
+        store(1, 2)
         join_sum(2)
         minimum(3, 3, s33)
         exponential(3, 3, s33)
         join_inverse(2)
+        divide(nc.vector, 1, 3)
+        store(1, 3)
         row_min(3)
         join_factors(3)
         divide(nc.vector, 2, 0)
+        store(2, 0)
         divide(nc.vector, 2, 1)
-        store(2, 0, banks=2)
+        store(2, 1)
         divide(nc.vector, 2, 2)
+        store(2, 2)
         divide(nc.vector, 2, 3)
-        store(2, 2, banks=2)
+        store(2, 3)
         join_sum(3)
         join_inverse(3)
         divide(nc.vector, 3, 0)

import concourse.mybir as mybir
from concourse.masks import make_identity

F32 = mybir.dt.float32
BF16 = mybir.dt.bfloat16
U32 = mybir.dt.uint32
U8 = mybir.dt.uint8
FP8X4 = mybir.dt.float8_e4m3fn_x4
ALU = mybir.AluOpType
ACT = mybir.ActivationFunctionType
AXIS_X = mybir.AxisListType.X

P = 128
TOKENS = 512
D_IN = 1024
D_KEY = 512
SLOTS = 2048
K_PASS = 512
N_PASS = 512
TOKEN_TILES = TOKENS // P
X_PASSES = D_IN // K_PASS
SLOT_TILES = SLOTS // P
CHUNKS = SLOTS // N_PASS
TILES_PER_CHUNK = N_PASS // P
EPS = 1e-12

FLOPS = 2 * TOKENS * D_IN * D_KEY + 2 * TOKENS * D_KEY * SLOTS


def tile_contentaddressablewritehead_pa_kernel(tc, controller_output, Wk, bk, memory, out):
    nc = tc.nc
    x_rows = controller_output.flatten_outer_dims()
    out_rows = out.flatten_outer_dims()

    with tc.tile_pool(name="keep", bufs=1) as keep, tc.tile_pool(name="junk", bufs=4) as junk, tc.psum_pool(
        name="psum", bufs=8
    ) as psum, tc.manual_schedule():

        warm = keep.tile([P, 2], F32)
        ident = keep.tile([P, P], F32)
        ones = keep.tile([P, P], BF16)
        minus_half = keep.tile([P, TILES_PER_CHUNK], F32)
        bias_rows = keep.tile([P, D_KEY], BF16)
        neg_bias = keep.tile([P, D_KEY], F32)

        x_sb = keep.tile([P, TOKEN_TILES, D_IN], BF16)
        x_grouped = keep.tile([P, TOKEN_TILES, X_PASSES, P, 2], F32, align_bytes=64)
        x_codes = keep.tile([P, TOKEN_TILES, X_PASSES * P], U32, align_bytes=64)
        x_scales = keep.tile([P, TOKEN_TILES, X_PASSES * P], U8, align_bytes=64)

        w_raw = keep.tile([P, X_PASSES, 4, D_KEY], BF16)
        w_grouped = keep.tile([P, X_PASSES, D_KEY, 4], BF16, align_bytes=64)
        w_codes = keep.tile([P, X_PASSES, D_KEY], U32, align_bytes=64)
        w_scales = keep.tile([P, X_PASSES, D_KEY], U8, align_bytes=64)

        neg_z = keep.tile([P, TOKEN_TILES, D_KEY], F32)
        neg_z_min = keep.tile([P, TOKEN_TILES], F32)
        e_key = keep.tile([P, TOKEN_TILES, D_KEY], F32)
        k_sumsq = keep.tile([P, TOKEN_TILES], F32)
        k_rnorm = keep.tile([P, TOKEN_TILES], F32)
        kn = keep.tile([P, TOKEN_TILES, D_KEY], BF16)
        k_grouped = keep.tile([P, TOKEN_TILES, P, 2], F32, align_bytes=64)
        k_codes = keep.tile([P, TOKEN_TILES, P], U32, align_bytes=64)
        k_scales = keep.tile([P, TOKEN_TILES, P], U8, align_bytes=64)

        mem_sb = keep.tile([P, SLOT_TILES, D_KEY], BF16)
        m_sumsq = keep.tile([P, SLOT_TILES], F32)
        m_floor = keep.tile([P, SLOT_TILES], F32)
        m_rnorm = keep.tile([P, SLOT_TILES], F32)
        mn = keep.tile([P, SLOT_TILES, D_KEY], BF16)
        m_grouped = keep.tile([P, SLOTS, 2], F32, align_bytes=64)
        m_codes = keep.tile([P, SLOTS], U32, align_bytes=64)
        m_scales = keep.tile([P, SLOTS], U8, align_bytes=64)

        bank_min = keep.tile([P, TOKEN_TILES, CHUNKS], F32)
        sims_min = keep.tile([P, TOKEN_TILES], F32)
        bank_sum = keep.tile([P, TOKEN_TILES, CHUNKS], F32)
        bank_factor = keep.tile([P, TOKEN_TILES, CHUNKS], F32)
        bank_part = keep.tile([P, TOKEN_TILES, CHUNKS], F32)
        row_sum = keep.tile([P, TOKEN_TILES], F32)
        inv_sum = keep.tile([P, TOKEN_TILES], F32)
        e_out = keep.tile([P, TOKEN_TILES, SLOTS], F32)
        w_out = keep.tile([P, TOKEN_TILES, SLOTS], F32)

        nc.vector.memset(warm[:], 0.0)
        nc.scalar.activation(out=warm[:, 1:2], in_=warm[:, 0:1], func=ACT.Exp)
        nc.vector.memset(bias_rows[:], 0.0)
        nc.vector.memset(ones[:], 1.0)
        make_identity(nc, ident[:])
        nc.gpsimd.memset(minus_half[:], -0.5)

        def load_weights(g):
            nc.sync.dma_start(
                out=w_raw[:, g].rearrange("p (u e) c -> p u e c", u=2),
                in_=Wk[K_PASS * g : K_PASS * (g + 1), :].rearrange("(u p e) c -> p u e c", u=2, e=2),
            )

        def load_memory(first, tiles):
            c, j = divmod(first, TILES_PER_CHUNK)
            chunk = memory[N_PASS * c : N_PASS * (c + 1), :].rearrange("(p j) m -> p j m", j=TILES_PER_CHUNK)
            nc.sync.dma_start(out=mem_sb[:, first : first + tiles, :], in_=chunk[:, j : j + tiles, :])

        def load_tokens(i):
            nc.sync.dma_start(out=x_sb[:, i, :], in_=x_rows[P * i : P * (i + 1), :])

        def load_bias():
            nc.sync.dma_start(out=bias_rows[0:1, :], in_=bk.unsqueeze(0))

        load_memory(0, 2)
        load_weights(0)
        load_bias()
        load_tokens(0)
        load_weights(1)
        load_tokens(1)
        load_memory(2, 2)
        load_tokens(2)
        load_tokens(3)
        load_memory(4, 4)
        load_memory(8, 4)
        load_memory(12, 4)

        def bias_matmul():
            bias_ps = psum.tile([P, D_KEY], F32, tag="bank")
            nc.tensor.matmul(bias_ps[:], lhsT=ones[:], rhs=bias_rows[:], start=True, stop=True)
            return bias_ps

        def bias_negate(bias_ps):
            nc.scalar.mul(out=neg_bias[:], in_=bias_ps[:], mul=-1.0)

        def weights_group(g):
            nc.vector.tensor_copy(
                out=w_grouped[:, g].rearrange("p (c i) t -> p c t i", i=4),
                in_=w_raw[:, g].rearrange("p t (c i) -> p c t i", i=4),
            )

        def weights_quantise(g):
            nc.vector.quantize_mx(
                out=w_codes[:, g, :].bitcast(FP8X4),
                scales=w_scales[:, g, :],
                in_=w_grouped[:, g].rearrange("p c t -> p (c t)"),
            )

        def tokens_transpose(i):
            x_words = x_sb[:, i, :].bitcast(F32)
            x_t = psum.tile([P, X_PASSES, 2, P], F32, tag="bank")
            for g in range(X_PASSES):
                for u in range(2):
                    first = 256 * g + P * u
                    nc.tensor.transpose(x_t[:, g, u, :], x_words[:, first : first + P], ident[:])
            return x_t

        def tokens_regroup(i, x_t):
            nc.scalar.copy(out=x_grouped[:, i], in_=x_t[:].rearrange("p g u r -> p g r u"))

        def tokens_quantise(i):
            nc.vector.quantize_mx(
                out=x_codes[:, i, :].bitcast(FP8X4),
                scales=x_scales[:, i, :],
                in_=x_grouped[:, i].rearrange("p g r u -> p (g r u)").bitcast(BF16),
            )

        def memory_lengths(pair):
            tiles = slice(2 * pair, 2 * pair + 2)
            for n in range(2 * pair, 2 * pair + 2):
                m_squares = junk.tile([P, D_KEY], BF16)
                nc.scalar.activation(
                    out=m_squares[:], in_=mem_sb[:, n, :], func=ACT.Square, accum_out=m_sumsq[:, n : n + 1]
                )
            nc.gpsimd.tensor_scalar(out=m_floor[:, tiles], in0=m_sumsq[:, tiles], scalar1=EPS, scalar2=None, op0=ALU.max)
            nc.gpsimd.tensor_tensor(out=m_rnorm[:, tiles], in0=m_floor[:, tiles], in1=minus_half[:, 0:2], op=ALU.pow)

        def memory_scale(pair):
            for n in range(2 * pair, 2 * pair + 2):
                nc.vector.tensor_scalar(
                    out=mn[:, n, :], in0=mem_sb[:, n, :], scalar1=m_rnorm[:, n : n + 1], scalar2=None, op0=ALU.mult
                )

        def memory_transpose(pair):
            m_t = psum.tile([P, 2, 2, P], F32, tag="bank")
            for j in range(2):
                mn_words = mn[:, 2 * pair + j, :].bitcast(F32)
                for u in range(2):
                    nc.tensor.transpose(m_t[:, j, u, :], mn_words[:, P * u : P * (u + 1)], ident[:])
            return m_t

        def memory_regroup(copy, pair, m_t):
            c, half = divmod(pair, 2)
            slots = m_grouped[:, N_PASS * c : N_PASS * (c + 1), :].rearrange("p (r j) u -> p r j u", j=TILES_PER_CHUNK)
            copy(out=slots[:, :, 2 * half : 2 * half + 2, :], in_=m_t[:].rearrange("p j u r -> p r j u"))

        def memory_quantise(c):
            slots = slice(N_PASS * c, N_PASS * (c + 1))
            nc.vector.quantize_mx(
                out=m_codes[:, slots].bitcast(FP8X4),
                scales=m_scales[:, slots],
                in_=m_grouped[:, slots, :].rearrange("p s u -> p (s u)").bitcast(BF16),
            )

        def key_matmul(i):
            z_ps = psum.tile([P, D_KEY], F32, tag="bank")
            for g in range(X_PASSES):
                nc.tensor.matmul_mx(
                    out=z_ps[:],
                    lhsT=x_codes[:, i, P * g : P * (g + 1)].bitcast(FP8X4),
                    lhsT_scale=x_scales[:, i, P * g : P * (g + 1)],
                    rhs=w_codes[:, g, :].bitcast(FP8X4),
                    rhs_scale=w_scales[:, g, :],
                    start=(g == 0),
                    stop=(g == X_PASSES - 1),
                )
            return z_ps

        def key_shift(i, z_ps):
            nc.vector.tensor_tensor(out=neg_z[:, i, :], in0=neg_bias[:], in1=z_ps[:], op=ALU.subtract)

        def key_min(i):
            nc.vector.tensor_reduce(out=neg_z_min[:, i : i + 1], in_=neg_z[:, i, :], axis=AXIS_X, op=ALU.min)

        def key_exp(i):
            nc.scalar.activation(
                out=e_key[:, i, :], in_=neg_z[:, i, :], func=ACT.Exp, bias=neg_z_min[:, i : i + 1], scale=-1.0
            )

        def key_length(i):
            e_squares = junk.tile([P, D_KEY], F32)
            nc.scalar.activation(out=e_squares[:], in_=e_key[:, i, :], func=ACT.Square, accum_out=k_sumsq[:, i : i + 1])

        def key_rnorm(i):
            nc.gpsimd.tensor_tensor(
                out=k_rnorm[:, i : i + 1], in0=k_sumsq[:, i : i + 1], in1=minus_half[:, 0:1], op=ALU.pow
            )

        def key_scale(i):
            nc.vector.tensor_scalar(
                out=kn[:, i, :], in0=e_key[:, i, :], scalar1=k_rnorm[:, i : i + 1], scalar2=None, op0=ALU.mult
            )

        def key_transpose(i):
            kn_words = kn[:, i, :].bitcast(F32)
            k_t = psum.tile([P, 2, P], F32, tag="bank")
            for u in range(2):
                nc.tensor.transpose(k_t[:, u, :], kn_words[:, P * u : P * (u + 1)], ident[:])
            return k_t

        def key_regroup(copy, i, k_t):
            copy(out=k_grouped[:, i], in_=k_t[:].rearrange("p u r -> p r u"))

        def key_quantise(i):
            nc.vector.quantize_mx(
                out=k_codes[:, i, :].bitcast(FP8X4),
                scales=k_scales[:, i, :],
                in_=k_grouped[:, i].rearrange("p r u -> p (r u)").bitcast(BF16),
            )

        def similarity(i, c):
            sims_ps = psum.tile([P, N_PASS], F32, tag="bank")
            nc.tensor.matmul_mx(
                out=sims_ps[:],
                lhsT=k_codes[:, i, :].bitcast(FP8X4),
                lhsT_scale=k_scales[:, i, :],
                rhs=m_codes[:, N_PASS * c : N_PASS * (c + 1)].bitcast(FP8X4),
                rhs_scale=m_scales[:, N_PASS * c : N_PASS * (c + 1)],
                start=True,
                stop=True,
            )
            return sims_ps

        def minimum(i, c, sims_ps):
            nc.vector.tensor_reduce(out=bank_min[:, i, c : c + 1], in_=sims_ps[:], axis=AXIS_X, op=ALU.min)

        def exponential(i, c, sims_ps):
            nc.scalar.activation(
                out=e_out[:, i, N_PASS * c : N_PASS * (c + 1)],
                in_=sims_ps[:],
                func=ACT.Exp,
                bias=bank_min[:, i, c : c + 1],
                scale=-1.0,
                accum_out=bank_sum[:, i, c : c + 1],
            )

        def row_min(i):
            nc.vector.tensor_reduce(out=sims_min[:, i : i + 1], in_=bank_min[:, i, :], axis=AXIS_X, op=ALU.min)

        def join_factors(i):
            nc.scalar.activation(
                out=bank_factor[:, i, :], in_=bank_min[:, i, :], func=ACT.Exp, bias=sims_min[:, i : i + 1], scale=-1.0
            )

        def join_sum(i):
            nc.vector.scalar_tensor_tensor(
                out=bank_part[:, i, :],
                in0=bank_sum[:, i, :],
                scalar=1.0,
                in1=bank_factor[:, i, :],
                op0=ALU.mult,
                op1=ALU.mult,
                accum_out=row_sum[:, i : i + 1],
            )

        def join_inverse(i):
            nc.vector.reciprocal(out=inv_sum[:, i : i + 1], in_=row_sum[:, i : i + 1])

        def divide(engine, i, c):
            cols = slice(N_PASS * c, N_PASS * (c + 1))
            engine.tensor_scalar(
                out=w_out[:, i, cols],
                in0=e_out[:, i, cols],
                scalar1=bank_factor[:, i, c : c + 1],
                scalar2=inv_sum[:, i : i + 1],
                op0=ALU.mult,
                op1=ALU.mult,
            )

        def store(i, c, banks=1):
            cols = slice(N_PASS * c, N_PASS * (c + banks))
            nc.sync.dma_start(out=out_rows[P * i : P * (i + 1), cols], in_=w_out[:, i, cols])

        on_vector, on_scalar = nc.vector.tensor_copy, nc.scalar.copy

        bias_ps = bias_matmul()
        x0 = tokens_transpose(0)
        x1 = tokens_transpose(1)
        x2 = tokens_transpose(2)
        x3 = tokens_transpose(3)
        weights_group(0)
        memory_lengths(0)
        memory_scale(0)
        bias_negate(bias_ps)
        weights_group(1)
        tokens_regroup(0, x0)
        weights_quantise(0)
        memory_lengths(1)
        tokens_quantise(0)
        tokens_regroup(1, x1)
        weights_quantise(1)
        tokens_regroup(2, x2)
        z0 = key_matmul(0)
        tokens_quantise(1)
        memory_lengths(2)
        z1 = key_matmul(1)
        m0 = memory_transpose(0)
        memory_scale(1)
        tokens_regroup(3, x3)
        tokens_quantise(2)
        memory_lengths(3)
        z2 = key_matmul(2)
        m1 = memory_transpose(1)
        key_shift(0, z0)
        memory_lengths(4)
        key_shift(1, z1)
        memory_lengths(5)
        key_min(0)
        key_exp(0)
        tokens_quantise(3)
        z3 = key_matmul(3)
        key_min(1)
        key_exp(1)
        key_shift(2, z2)
        key_length(0)
        key_rnorm(0)
        memory_scale(2)
        key_length(1)
        key_rnorm(1)
        m2 = memory_transpose(2)
        key_min(2)
        memory_lengths(6)
        key_shift(3, z3)
        memory_lengths(7)
        memory_scale(3)
        key_exp(2)
        m3 = memory_transpose(3)
        key_min(3)
        key_exp(3)
        memory_regroup(on_vector, 0, m0)
        key_length(2)
        key_rnorm(2)
        memory_regroup(on_vector, 1, m1)
        key_length(3)
        key_rnorm(3)
        memory_scale(4)
        m4 = memory_transpose(4)
        memory_quantise(0)
        memory_scale(5)
        m5 = memory_transpose(5)
        memory_regroup(on_vector, 2, m2)
        memory_regroup(on_vector, 3, m3)
        key_scale(0)
        k0 = key_transpose(0)
        key_scale(1)
        key_regroup(on_scalar, 0, k0)
        k1 = key_transpose(1)
        memory_quantise(1)
        key_regroup(on_scalar, 1, k1)
        memory_scale(6)
        m6 = memory_transpose(6)
        memory_regroup(on_vector, 4, m4)
        memory_regroup(on_scalar, 6, m6)
        memory_scale(7)
        m7 = memory_transpose(7)
        memory_regroup(on_vector, 5, m5)
        memory_regroup(on_scalar, 7, m7)
        key_quantise(0)
        s00 = similarity(0, 0)
        s01 = similarity(0, 1)
        memory_quantise(2)
        key_quantise(1)
        key_scale(2)
        k2 = key_transpose(2)
        s02 = similarity(0, 2)
        minimum(0, 0, s00)
        exponential(0, 0, s00)
        key_scale(3)
        key_regroup(on_scalar, 2, k2)
        k3 = key_transpose(3)
        minimum(0, 1, s01)
        exponential(0, 1, s01)
        memory_quantise(3)
        key_regroup(on_scalar, 3, k3)
        s03 = similarity(0, 3)
        s10 = similarity(1, 0)
        s11 = similarity(1, 1)
        s12 = similarity(1, 2)
        s13 = similarity(1, 3)
        minimum(0, 2, s02)
        exponential(0, 2, s02)
        key_quantise(2)
        s20 = similarity(2, 0)
        s21 = similarity(2, 1)
        s22 = similarity(2, 2)
        s23 = similarity(2, 3)
        minimum(0, 3, s03)
        exponential(0, 3, s03)
        key_quantise(3)
        s30 = similarity(3, 0)
        s31 = similarity(3, 1)
        s32 = similarity(3, 2)
        s33 = similarity(3, 3)
        minimum(1, 0, s10)
        row_min(0)
        join_factors(0)
        minimum(1, 1, s11)
        exponential(1, 0, s10)
        minimum(1, 2, s12)
        exponential(1, 1, s11)
        join_sum(0)
        exponential(1, 2, s12)
        minimum(1, 3, s13)
        exponential(1, 3, s13)
        join_inverse(0)
        divide(nc.gpsimd, 0, 0)
        store(0, 0)
        minimum(2, 0, s20)
        divide(nc.gpsimd, 0, 1)
        store(0, 1)
        row_min(1)
        join_factors(1)
        divide(nc.gpsimd, 0, 2)
        store(0, 2)
        minimum(2, 1, s21)
        exponential(2, 0, s20)
        divide(nc.gpsimd, 0, 3)
        store(0, 3)
        minimum(2, 2, s22)
        exponential(2, 1, s21)
        minimum(2, 3, s23)
        exponential(2, 2, s22)
        join_sum(1)
        exponential(2, 3, s23)
        minimum(3, 0, s30)
        join_inverse(1)
        row_min(2)
        join_factors(2)
        minimum(3, 1, s31)
        exponential(3, 0, s30)
        divide(nc.vector, 1, 0)
        exponential(3, 1, s31)
        store(1, 0)
        divide(nc.vector, 1, 1)
        store(1, 1)
        minimum(3, 2, s32)
        exponential(3, 2, s32)
        divide(nc.vector, 1, 2)
        store(1, 2)
        join_sum(2)
        minimum(3, 3, s33)
        exponential(3, 3, s33)
        join_inverse(2)
        divide(nc.vector, 1, 3)
        store(1, 3)
        row_min(3)
        join_factors(3)
        divide(nc.vector, 2, 0)
        store(2, 0)
        divide(nc.vector, 2, 1)
        store(2, 1)
        divide(nc.vector, 2, 2)
        store(2, 2)
        divide(nc.vector, 2, 3)
        store(2, 3)
        join_sum(3)
        join_inverse(3)
        divide(nc.vector, 3, 0)
        store(3, 0)
        divide(nc.vector, 3, 1)
        store(3, 1)
        divide(nc.vector, 3, 2)
        store(3, 2)
        divide(nc.vector, 3, 3)
        store(3, 3)
